import numpy as np
import ml_dtypes


def mxq(x, axis, fmt="e4m3"):
    dtype, down = {"e4m3": (ml_dtypes.float8_e4m3fn, 7), "e5m2": (ml_dtypes.float8_e5m2, 14)}[fmt]
    v = np.moveaxis(np.asarray(x, np.float32).astype(ml_dtypes.bfloat16).astype(np.float64), axis, -1)
    blocks = v.reshape(v.shape[:-1] + (-1, 32))
    amax = np.abs(blocks).max(-1, keepdims=True)
    byte = np.maximum(np.where(amax > 0, np.frexp(amax)[1] - 1 + 127, 0) - down, 1)
    scale = np.exp2(byte - 127.0)
    codes = (blocks / scale).astype(np.float32).astype(dtype).astype(np.float64)
    return np.moveaxis((codes * scale).reshape(v.shape), -1, axis)


WIDE = False


def mx_kscale(k):
    if not WIDE:
        return np.ones(k)
    levels = np.array([10, -10, 5, -5, 0])
    if k % 512:
        return np.exp2(np.random.permutation(np.resize(levels, k // 32))).repeat(32)
    a = np.empty((k // 512, 16))
    for p in range(k // 512):
        a[p, :8] = np.random.permutation(np.resize(levels, 8))
        for g in range(8):
            far = levels[np.abs(levels - a[p, g]) >= 10]
            a[p, g + 8] = far[np.random.randint(len(far))]
    return np.exp2(a.ravel()).repeat(32)


BF16 = ml_dtypes.bfloat16


def bf(x):
    return np.asarray(x, np.float32).astype(BF16)


def f64(x):
    return np.asarray(x).astype(np.float64)


E2M1 = np.array([0.0, 0.5, 1.0, 1.5, 2.0, 3.0, 4.0, 6.0, -0.0, -0.5, -1.0, -1.5, -2.0, -3.0, -4.0, -6.0])


def pack_weight(w, fmt):
    k, n = w.shape
    w = f64(bf(w)).reshape(k // 32, 32, n)
    amax = np.abs(w).max(1)
    if fmt == "e4m3":
        byte = np.frexp(amax)[1] - 1 + 127 - 7
    else:
        mant, ex = np.frexp(amax / 6.0)
        byte = np.where(mant > 0.5, ex, ex - 1) + 127
    byte = np.clip(np.where(amax > 0, byte, 1), 1, 254)
    scaled = (w * np.exp2(127.0 - byte)[:, None, :]).reshape(k, n).astype(np.float32)
    by_word = np.ascontiguousarray(scaled.reshape(k // 512, 128, 4, n).transpose(0, 1, 3, 2))
    if fmt == "e4m3":
        words = by_word.astype(ml_dtypes.float8_e4m3fn).view(np.uint8)
    else:
        c = by_word.astype(ml_dtypes.float4_e2m1fn).view(np.uint8) & 0xF
        words = c[..., 0::2] | (c[..., 1::2] << 4)
    return np.ascontiguousarray(words), np.ascontiguousarray(byte.astype(np.uint8).reshape(k // 512, 16, n))


def unpack_weight(words, scales, fmt):
    g, p, n, _ = words.shape
    if fmt == "e4m3":
        vals = np.ascontiguousarray(words).view(ml_dtypes.float8_e4m3fn).astype(np.float64)
    else:
        nib = np.empty((g, p, n, 4), np.uint8)
        nib[..., 0::2] = words & 0xF
        nib[..., 1::2] = words >> 4
        vals = E2M1[nib]
    vals = vals * np.repeat(np.exp2(scales.astype(np.float64) - 127.0), 8, axis=1)[..., None]
    return vals.transpose(0, 1, 3, 2).reshape(g * 512, n)


N, E, C = 2048, 1024, 512
DENSITY = 0.01
HE_RMS = np.sqrt(np.e / E)


def setup_inputs():
    s, t = mx_kscale(E), mx_kscale(C)
    member = np.random.uniform(size=(N, E)) < DENSITY
    incidence = bf(member * s[None, :])
    he = bf(np.random.standard_normal((E, C)) * HE_RMS / s[:, None] * t[None, :])
    W2_words, W2_scales = pack_weight(np.random.standard_normal((C, C)) * 3.0 / np.sqrt(C) / t[:, None], "e4m3")
    return {"incidence": incidence,
            "he": he,
            "W2_words": W2_words,
            "W2_scales": W2_scales,
            "b2": bf(np.random.standard_normal(C) * 0.2),
            "node_features": bf(np.random.standard_normal((N, C)))}


def reference(incidence, he, W2_words, W2_scales, b2, node_features):
    prop = mxq(f64(incidence), 1, "e4m3") @ mxq(f64(he), 0, "e4m3")
    return (mxq(prop, 1, "e4m3") @ unpack_weight(W2_words, W2_scales, "e4m3")) + f64(b2) + f64(node_features)

@@ -1,0 +1,204 @@
+from contextlib import ExitStack
+
+import concourse.mybir as mybir
+from concourse.masks import make_identity
+
+BF16 = mybir.dt.bfloat16
+F32 = mybir.dt.float32
+I32 = mybir.dt.int32
+U32 = mybir.dt.uint32
+U8 = mybir.dt.uint8
+FP8X4 = mybir.dt.float8_e4m3fn_x4
+ADD = mybir.AluOpType.add
+
+P = 128
+PACK = 4
+K_PASS = P * PACK
+
+NODES, EDGES, CHANNELS = 2048, 1024, 512
+EDGE_PASSES = EDGES // K_PASS
+BLOCK = P
+CHUNK_BLOCKS = 4
+UNIT_BLOCKS = 2
+CHUNKS = NODES // (CHUNK_BLOCKS * BLOCK)
+UNITS = NODES // (UNIT_BLOCKS * BLOCK)
+UNITS_PER_CHUNK = CHUNK_BLOCKS // UNIT_BLOCKS
+
+FLOPS = 2 * NODES * EDGES * CHANNELS + 2 * NODES * CHANNELS * CHANNELS
+
+
+def tile_heterogeneoustemporalhypergraphnn_pb_kernel(
+    tc, incidence, he, W2_words, W2_scales, b2, node_features, out
+):
+    nc = tc.nc
+    with ExitStack() as ctx:
+        ctx.enter_context(tc.manual_schedule())
+        keep = ctx.enter_context(tc.tile_pool(name="keep", bufs=1))
+        inc_pool = ctx.enter_context(tc.tile_pool(name="inc", bufs=UNITS))
+        nf_pool = ctx.enter_context(tc.tile_pool(name="nf", bufs=CHUNKS))
+        work = ctx.enter_context(tc.tile_pool(name="work", bufs=3))
+        late = ctx.enter_context(tc.tile_pool(name="late", bufs=4))
+        psum_t = ctx.enter_context(tc.psum_pool(name="psum_t", bufs=2))
+        psum_p = ctx.enter_context(tc.psum_pool(name="psum_p", bufs=2))
+        psum_o = ctx.enter_context(tc.psum_pool(name="psum_o", bufs=4))
+
+        inc_v = incidence.rearrange("(c p j) e -> c p j e", p=P, j=CHUNK_BLOCKS)
+        nf_v = node_features.rearrange("(c p j) n -> c p j n", p=P, j=CHUNK_BLOCKS)
+        out_v = out.rearrange("(c p j) n -> c p j n", p=P, j=CHUNK_BLOCKS)
+        he_v = he.rearrange("(g p t) n -> g p t n", g=EDGE_PASSES, p=P, t=PACK)
+
+        ident = keep.tile([P, P], F32)
+        make_identity(nc, ident[:])
+        ones = keep.tile([P, P], BF16)
+        nc.vector.memset(ones[:], 1.0)
+        bias_row = keep.tile([P, CHANNELS], BF16)
+        nc.vector.memset(bias_row[:], 0.0)
+        w2_plane = keep.tile([P, CHANNELS], U8, align_bytes=64)
+        nc.vector.memset(w2_plane[:].bitcast(I32), 0)
+
+        he_raw = keep.tile([P, EDGE_PASSES, PACK, CHANNELS], BF16)
+        for g in range(EDGE_PASSES):
+            nc.sync.dma_start(out=he_raw[:, g], in_=he_v[g])
+        nc.sync.dma_start(out=bias_row[0:1, :], in_=b2.rearrange("(o n) -> o n", o=1))
+        w2_codes = keep.tile([P, CHANNELS], U32, align_bytes=64)
+        inc_of = {}
+        nf_of = {}
+        for c in range(CHUNKS):
+            for h in range(UNITS_PER_CHUNK):
+                inc_sb = inc_pool.tile([P, UNIT_BLOCKS, EDGES], BF16)
+                rows = slice(h * UNIT_BLOCKS, (h + 1) * UNIT_BLOCKS)
+                nc.sync.dma_start(out=inc_sb[:], in_=inc_v[c][:, rows, :])
+                inc_of[c * UNITS_PER_CHUNK + h] = inc_sb
+            if c == 0:
+                nc.sync.dma_start(
+                    out=w2_codes[:].bitcast(I32),
+                    in_=W2_words[0].rearrange("p n t -> p (n t)").bitcast(I32),
+                )
+                for quad in range(4):
+                    nc.sync.dma_start(
+                        out=w2_plane[32 * quad : 32 * quad + 4, :].bitcast(I32),
+                        in_=W2_scales[0][4 * quad : 4 * quad + 4, :].bitcast(I32),
+                    )
+            nf_sb = nf_pool.tile([P, CHUNK_BLOCKS, CHANNELS], BF16)
+            nc.sync.dma_start(out=nf_sb[:], in_=nf_v[c])
+            nf_of[c] = nf_sb
+
+        bias_ps = psum_o.tile([P, CHANNELS], F32, tag="second")
+        nc.tensor.matmul(out=bias_ps[:], lhsT=ones[:], rhs=bias_row[:], start=True, stop=True)
+        bias_all = keep.tile([P, CHANNELS], F32)
+        nc.scalar.copy(out=bias_all[:], in_=bias_ps[:])
+
+        he_grouped = keep.tile([P, EDGE_PASSES, PACK, P, PACK], BF16, align_bytes=64)
+        he_codes = keep.tile([P, EDGE_PASSES, CHANNELS], U32, align_bytes=64)
+        he_scales = keep.tile([P, EDGE_PASSES, CHANNELS], U8, align_bytes=64)
+        for g in range(EDGE_PASSES):
+            nc.vector.tensor_copy(
+                out=he_grouped[:, g],
+                in_=he_raw[:, g].rearrange("p t (m q) -> p q m t", q=PACK),
+            )
+        for g in range(EDGE_PASSES):
+            nc.vector.quantize_mx(
+                out=he_codes[:, g, :].bitcast(FP8X4),
+                scales=he_scales[:, g, :],
+                in_=he_grouped[:, g].rearrange("p q m t -> p (q m t)"),
+            )
+
+        inc_q = {}
+        prop_q = {}
+        base_of = {}
+
+        def transpose_and_quantise(u):
+            grouped = work.tile([P, UNIT_BLOCKS, EDGE_PASSES, BLOCK, PACK], BF16, align_bytes=64)
+            for a in range(UNIT_BLOCKS):
+                words = inc_of[u][:, a, :].bitcast(F32)
+                flipped = psum_t.tile([P, EDGE_PASSES * 2, BLOCK], F32)
+                for g in range(EDGE_PASSES):
+                    for v in range(2):
+                        nc.tensor.transpose(
+                            flipped[:, 2 * g + v, :],
+                            words[:, 2 * P * g + v : 2 * P * (g + 1) : 2],
+                            ident[:],
+                        )
+                nc.scalar.copy(
+                    out=grouped[:, a].bitcast(F32),
+                    in_=flipped[:].rearrange("p (g u) n -> p g n u", u=2),
+                )
+            codes = work.tile([P, UNIT_BLOCKS, EDGE_PASSES, BLOCK], U32, align_bytes=64)
+            scales = work.tile([P, UNIT_BLOCKS, EDGE_PASSES, BLOCK], U8, align_bytes=64)
+            nc.vector.quantize_mx(
+                out=codes[:].rearrange("p a g n -> p (a g n)").bitcast(FP8X4),
+                scales=scales[:].rearrange("p a g n -> p (a g n)"),
+                in_=grouped[:].rearrange("p a g n t -> p (a g n t)"),
+            )
+            inc_q[u] = (codes, scales)
+
+        def add_bias_to_residual(u):
+            base = late.tile([P, UNIT_BLOCKS, CHANNELS], F32)
+            first = (u % UNITS_PER_CHUNK) * UNIT_BLOCKS
+            nc.vector.tensor_tensor(
+                out=base[:],
+                in0=nf_of[u // UNITS_PER_CHUNK][:, first : first + UNIT_BLOCKS, :],
+                in1=bias_all[:].unsqueeze(1).to_broadcast([P, UNIT_BLOCKS, CHANNELS]),
+                op=ADD,
+            )
+            base_of[u] = base
+
+        def first_product(u):
+            codes, scales = inc_q[u]
+            prop_grouped = work.tile([P, UNIT_BLOCKS, BLOCK, PACK], BF16, align_bytes=64)
+            for a in range(UNIT_BLOCKS):
+                prop_ps = psum_p.tile([P, PACK, BLOCK], F32)
+                for q in range(PACK):
+                    cols = slice(q * P, (q + 1) * P)
+                    for g in range(EDGE_PASSES):
+                        nc.tensor.matmul_mx(
+                            out=prop_ps[:, q, :],
+                            lhsT=he_codes[:, g, cols].bitcast(FP8X4),
+                            lhsT_scale=he_scales[:, g, cols],
+                            rhs=codes[:, a, g, :].bitcast(FP8X4),
+                            rhs_scale=scales[:, a, g, :],
+                            start=(g == 0),
+                            stop=(g == EDGE_PASSES - 1),
+                        )
+                nc.scalar.copy(
+                    out=prop_grouped[:, a], in_=prop_ps[:].rearrange("p q n -> p n q")
+                )
+            prop_codes = work.tile([P, UNIT_BLOCKS, BLOCK], U32, align_bytes=64)
+            prop_scales = work.tile([P, UNIT_BLOCKS, BLOCK], U8, align_bytes=64)
+            nc.vector.quantize_mx(
+                out=prop_codes[:].rearrange("p a n -> p (a n)").bitcast(FP8X4),
+                scales=prop_scales[:].rearrange("p a n -> p (a n)"),
+                in_=prop_grouped[:].rearrange("p a n t -> p (a n t)"),
+            )
+            prop_q[u] = (prop_codes, prop_scales)
+
+        def second_product(u):
+            prop_codes, prop_scales = prop_q[u]
+            result = late.tile([P, UNIT_BLOCKS, CHANNELS], F32)
+            for a in range(UNIT_BLOCKS):
+                second = psum_o.tile([P, CHANNELS], F32)
+                nc.tensor.matmul_mx(
+                    out=second[:],
+                    lhsT=prop_codes[:, a, :].bitcast(FP8X4),
+                    lhsT_scale=prop_scales[:, a, :],
+                    rhs=w2_codes[:].bitcast(FP8X4),
+                    rhs_scale=w2_plane[:],
+                    start=True,
+                    stop=True,
+                )
+                nc.vector.tensor_tensor(
+                    out=result[:, a, :], in0=second[:], in1=base_of[u][:, a, :], op=ADD
+                )
+            first = (u % UNITS_PER_CHUNK) * UNIT_BLOCKS
+            nc.sync.dma_start(
+                out=out_v[u // UNITS_PER_CHUNK][:, first : first + UNIT_BLOCKS, :], in_=result[:]
+            )
+
+        for k in range(UNITS + 2):
+            if k < UNITS:
+                transpose_and_quantise(k)
+                add_bias_to_residual(k)
+            if 1 <= k <= UNITS:
+                first_product(k - 1)
+            if k >= 2:
+                second_product(k - 2)

@@ -51,6 +51,8 @@ def tile_heterogeneoustemporalhypergraphnn_pb_kernel(
         make_identity(nc, ident[:])
         ones = keep.tile([P, P], BF16)
         nc.vector.memset(ones[:], 1.0)
+        zeros = keep.tile([P, CHANNELS], BF16)
+        nc.vector.memset(zeros[:], 0.0)
         bias_row = keep.tile([P, CHANNELS], BF16)
         nc.vector.memset(bias_row[:], 0.0)
         w2_plane = keep.tile([P, CHANNELS], U8, align_bytes=64)
@@ -82,6 +84,15 @@ def tile_heterogeneoustemporalhypergraphnn_pb_kernel(
             nf_sb = nf_pool.tile([P, CHUNK_BLOCKS, CHANNELS], BF16)
             nc.sync.dma_start(out=nf_sb[:], in_=nf_v[c])
             nf_of[c] = nf_sb
+
+        def warm_up(count):
+            for i in range(count):
+                idle = psum_o.tile([P, CHANNELS], F32, tag="second")
+                nc.tensor.matmul(
+                    out=idle[:], lhsT=ones[:], rhs=zeros[:], start=True, stop=True
+                )
+
+        warm_up(8)
 
         bias_ps = psum_o.tile([P, CHANNELS], F32, tag="second")
         nc.tensor.matmul(out=bias_ps[:], lhsT=ones[:], rhs=bias_row[:], start=True, stop=True)
@@ -197,6 +208,8 @@ def tile_heterogeneoustemporalhypergraphnn_pb_kernel(
         for k in range(UNITS + 2):
             if k < UNITS:
                 transpose_and_quantise(k)
+                if k < 2:
+                    warm_up(2)
                 add_bias_to_residual(k)
             if 1 <= k <= UNITS:
                 first_product(k - 1)

@@ -104,8 +104,8 @@ def tile_heterogeneoustemporalhypergraphnn_pb_kernel(
         he_scales = keep.tile([P, EDGE_PASSES, CHANNELS], U8, align_bytes=64)
         for g in range(EDGE_PASSES):
             nc.vector.tensor_copy(
-                out=he_grouped[:, g],
-                in_=he_raw[:, g].rearrange("p t (m q) -> p q m t", q=PACK),
+                out=he_grouped[:, g].rearrange("p q m t -> p m t q"),
+                in_=he_raw[:, g].rearrange("p t (m q) -> p m t q", q=PACK),
             )
         for g in range(EDGE_PASSES):
             nc.vector.quantize_mx(

@@ -47,93 +47,139 @@ def tile_heterogeneoustemporalhypergraphnn_pb_kernel(
         out_v = out.rearrange("(c p j) n -> c p j n", p=P, j=CHUNK_BLOCKS)
         he_v = he.rearrange("(g p t) n -> g p t n", g=EDGE_PASSES, p=P, t=PACK)
 
+        def part(view, u):
+            first = (u % UNITS_PER_CHUNK) * UNIT_BLOCKS
+            return view[u // UNITS_PER_CHUNK][:, first : first + UNIT_BLOCKS, :]
+
         ident = keep.tile([P, P], F32)
         make_identity(nc, ident[:])
         ones = keep.tile([P, P], BF16)
         nc.vector.memset(ones[:], 1.0)
-        zeros = keep.tile([P, CHANNELS], BF16)
-        nc.vector.memset(zeros[:], 0.0)
         bias_row = keep.tile([P, CHANNELS], BF16)
         nc.vector.memset(bias_row[:], 0.0)
         w2_plane = keep.tile([P, CHANNELS], U8, align_bytes=64)
         nc.vector.memset(w2_plane[:].bitcast(I32), 0)
 
         he_raw = keep.tile([P, EDGE_PASSES, PACK, CHANNELS], BF16)
-        for g in range(EDGE_PASSES):
-            nc.sync.dma_start(out=he_raw[:, g], in_=he_v[g])
-        nc.sync.dma_start(out=bias_row[0:1, :], in_=b2.rearrange("(o n) -> o n", o=1))
         w2_codes = keep.tile([P, CHANNELS], U32, align_bytes=64)
         inc_of = {}
         nf_of = {}
-        for c in range(CHUNKS):
-            for h in range(UNITS_PER_CHUNK):
-                inc_sb = inc_pool.tile([P, UNIT_BLOCKS, EDGES], BF16)
-                rows = slice(h * UNIT_BLOCKS, (h + 1) * UNIT_BLOCKS)
-                nc.sync.dma_start(out=inc_sb[:], in_=inc_v[c][:, rows, :])
-                inc_of[c * UNITS_PER_CHUNK + h] = inc_sb
-            if c == 0:
-                nc.sync.dma_start(
-                    out=w2_codes[:].bitcast(I32),
-                    in_=W2_words[0].rearrange("p n t -> p (n t)").bitcast(I32),
-                )
-                for quad in range(4):
-                    nc.sync.dma_start(
-                        out=w2_plane[32 * quad : 32 * quad + 4, :].bitcast(I32),
-                        in_=W2_scales[0][4 * quad : 4 * quad + 4, :].bitcast(I32),
-                    )
+
+        def load_incidence(u):
+            inc_sb = inc_pool.tile([P, UNIT_BLOCKS, EDGES], BF16)
+            nc.sync.dma_start(out=inc_sb[:], in_=part(inc_v, u))
+            inc_of[u] = inc_sb
+
+        def load_he(g):
+            nc.sync.dma_start(out=he_raw[:, g], in_=he_v[g])
+
+        def load_features(c):
             nf_sb = nf_pool.tile([P, CHUNK_BLOCKS, CHANNELS], BF16)
             nc.sync.dma_start(out=nf_sb[:], in_=nf_v[c])
-            nf_of[c] = nf_sb
+            for h in range(UNITS_PER_CHUNK):
+                nf_of[c * UNITS_PER_CHUNK + h] = nf_sb[:, h * UNIT_BLOCKS : (h + 1) * UNIT_BLOCKS, :]
 
-        def warm_up(count):
-            for i in range(count):
-                idle = psum_o.tile([P, CHANNELS], F32, tag="second")
-                nc.tensor.matmul(
-                    out=idle[:], lhsT=ones[:], rhs=zeros[:], start=True, stop=True
+        def load_weight():
+            nc.sync.dma_start(
+                out=w2_codes[:].bitcast(I32),
+                in_=W2_words[0].rearrange("p n t -> p (n t)").bitcast(I32),
+            )
+            for quad in range(4):
+                nc.sync.dma_start(
+                    out=w2_plane[32 * quad : 32 * quad + 4, :].bitcast(I32),
+                    in_=W2_scales[0][4 * quad : 4 * quad + 4, :].bitcast(I32),
                 )
 
-        warm_up(8)
+        def load_bias():
+            nc.sync.dma_start(out=bias_row[0:1, :], in_=b2.rearrange("(o n) -> o n", o=1))
 
-        bias_ps = psum_o.tile([P, CHANNELS], F32, tag="second")
-        nc.tensor.matmul(out=bias_ps[:], lhsT=ones[:], rhs=bias_row[:], start=True, stop=True)
+        load_he(0)
+        load_he(1)
+        load_bias()
+        for c in range(CHUNKS):
+            for h in range(UNITS_PER_CHUNK):
+                load_incidence(c * UNITS_PER_CHUNK + h)
+            if c == 0:
+                load_weight()
+            load_features(c)
+
+
         bias_all = keep.tile([P, CHANNELS], F32)
-        nc.scalar.copy(out=bias_all[:], in_=bias_ps[:])
+
+        def spread_bias():
+            bias_ps = psum_o.tile([P, CHANNELS], F32, tag="second")
+            nc.tensor.matmul(
+                out=bias_ps[:], lhsT=ones[:], rhs=bias_row[:], start=True, stop=True
+            )
+            nc.scalar.copy(out=bias_all[:], in_=bias_ps[:])
+
+        def warm_up(rows):
+            for row in rows:
+                idle = psum_o.tile([P, CHANNELS], F32, tag="second")
+                nc.tensor.matmul(out=idle[:], lhsT=ones[:], rhs=row, start=True, stop=True)
 
         he_grouped = keep.tile([P, EDGE_PASSES, PACK, P, PACK], BF16, align_bytes=64)
         he_codes = keep.tile([P, EDGE_PASSES, CHANNELS], U32, align_bytes=64)
         he_scales = keep.tile([P, EDGE_PASSES, CHANNELS], U8, align_bytes=64)
-        for g in range(EDGE_PASSES):
-            nc.vector.tensor_copy(
-                out=he_grouped[:, g].rearrange("p q m t -> p m t q"),
-                in_=he_raw[:, g].rearrange("p t (m q) -> p m t q", q=PACK),
-            )
-        for g in range(EDGE_PASSES):
-            nc.vector.quantize_mx(
-                out=he_codes[:, g, :].bitcast(FP8X4),
-                scales=he_scales[:, g, :],
-                in_=he_grouped[:, g].rearrange("p q m t -> p (q m t)"),
+
+        def group_he(g, first, last, copy):
+            copy(
+                out=he_grouped[:, g, first:last].rearrange("p q m t -> p m t q"),
+                in_=he_raw[:, g].rearrange("p t (m q) -> p m t q", q=PACK)[:, :, :, first:last],
             )
 
+        def quantise_he(g, first, last):
+            cols = slice(first * P, last * P)
+            nc.vector.quantize_mx(
+                out=he_codes[:, g, cols].bitcast(FP8X4),
+                scales=he_scales[:, g, cols],
+                in_=he_grouped[:, g, first:last].rearrange("p q m t -> p (q m t)"),
+            )
+
+        flipped_of = {}
+        grouped_of = {}
         inc_q = {}
+        prop_ps_of = {}
+        propg_of = {}
         prop_q = {}
         base_of = {}
+        second_of = {}
+        result_of = {}
 
-        def transpose_and_quantise(u):
-            grouped = work.tile([P, UNIT_BLOCKS, EDGE_PASSES, BLOCK, PACK], BF16, align_bytes=64)
+        reordered_of = {}
+
+        def reorder(u, a, copy):
+            sorted_words = work.tile([P, EDGE_PASSES, 2, P], F32)
+            copy(
+                out=sorted_words[:],
+                in_=inc_of[u][:, a, :].bitcast(F32).rearrange("p (g i v) -> p g v i", g=EDGE_PASSES, v=2),
+            )
+            reordered_of[u, a] = sorted_words
+
+        def transpose(u):
             for a in range(UNIT_BLOCKS):
                 words = inc_of[u][:, a, :].bitcast(F32)
                 flipped = psum_t.tile([P, EDGE_PASSES * 2, BLOCK], F32)
                 for g in range(EDGE_PASSES):
                     for v in range(2):
-                        nc.tensor.transpose(
-                            flipped[:, 2 * g + v, :],
-                            words[:, 2 * P * g + v : 2 * P * (g + 1) : 2],
-                            ident[:],
-                        )
+                        if (u, a) in reordered_of:
+                            source = reordered_of[u, a][:, g, v, :]
+                        else:
+                            source = words[:, 2 * P * g + v : 2 * P * (g + 1) : 2]
+                        nc.tensor.transpose(flipped[:, 2 * g + v, :], source, ident[:])
+                flipped_of[u, a] = flipped
+
+        def copy_incidence(u):
+            grouped = work.tile([P, UNIT_BLOCKS, EDGE_PASSES, BLOCK, PACK], BF16, align_bytes=64)
+            for a in range(UNIT_BLOCKS):
                 nc.scalar.copy(
                     out=grouped[:, a].bitcast(F32),
-                    in_=flipped[:].rearrange("p (g u) n -> p g n u", u=2),
+                    in_=flipped_of[u, a][:].rearrange("p (g u) n -> p g n u", u=2),
                 )
+            grouped_of[u] = grouped
+
+        def quantise_incidence(u):
+            grouped = grouped_of[u]
             codes = work.tile([P, UNIT_BLOCKS, EDGE_PASSES, BLOCK], U32, align_bytes=64)
             scales = work.tile([P, UNIT_BLOCKS, EDGE_PASSES, BLOCK], U8, align_bytes=64)
             nc.vector.quantize_mx(
@@ -145,19 +191,17 @@ def tile_heterogeneoustemporalhypergraphnn_pb_kernel(
 
         def add_bias_to_residual(u):
             base = late.tile([P, UNIT_BLOCKS, CHANNELS], F32)
-            first = (u % UNITS_PER_CHUNK) * UNIT_BLOCKS
             nc.vector.tensor_tensor(
                 out=base[:],
-                in0=nf_of[u // UNITS_PER_CHUNK][:, first : first + UNIT_BLOCKS, :],
+                in0=nf_of[u],
                 in1=bias_all[:].unsqueeze(1).to_broadcast([P, UNIT_BLOCKS, CHANNELS]),
                 op=ADD,
             )
             base_of[u] = base
 
-        def first_product(u):
+        def first_product(u, blocks=(0, 1)):
             codes, scales = inc_q[u]
-            prop_grouped = work.tile([P, UNIT_BLOCKS, BLOCK, PACK], BF16, align_bytes=64)
-            for a in range(UNIT_BLOCKS):
+            for a in blocks:
                 prop_ps = psum_p.tile([P, PACK, BLOCK], F32)
                 for q in range(PACK):
                     cols = slice(q * P, (q + 1) * P)
@@ -171,47 +215,100 @@ def tile_heterogeneoustemporalhypergraphnn_pb_kernel(
                             start=(g == 0),
                             stop=(g == EDGE_PASSES - 1),
                         )
-                nc.scalar.copy(
-                    out=prop_grouped[:, a], in_=prop_ps[:].rearrange("p q n -> p n q")
-                )
+                prop_ps_of[u, a] = prop_ps
+
+        def copy_prop(u):
+            open_prop(u)
+            for a in range(UNIT_BLOCKS):
+                copy_prop_block(u, a)
+
+        def copy_prop_block(u, a):
+            nc.scalar.copy(
+                out=propg_of[u][:, a],
+                in_=prop_ps_of[u, a][:].rearrange("p q n -> p n q"),
+            )
+
+        def open_prop(u):
+            prop_grouped = work.tile([P, UNIT_BLOCKS, BLOCK, PACK], BF16, align_bytes=64)
+            propg_of[u] = prop_grouped
             prop_codes = work.tile([P, UNIT_BLOCKS, BLOCK], U32, align_bytes=64)
             prop_scales = work.tile([P, UNIT_BLOCKS, BLOCK], U8, align_bytes=64)
-            nc.vector.quantize_mx(
-                out=prop_codes[:].rearrange("p a n -> p (a n)").bitcast(FP8X4),
-                scales=prop_scales[:].rearrange("p a n -> p (a n)"),
-                in_=prop_grouped[:].rearrange("p a n t -> p (a n t)"),
-            )
             prop_q[u] = (prop_codes, prop_scales)
 
-        def second_product(u):
+        def quantise_prop(u, first, last):
             prop_codes, prop_scales = prop_q[u]
-            result = late.tile([P, UNIT_BLOCKS, CHANNELS], F32)
-            for a in range(UNIT_BLOCKS):
-                second = psum_o.tile([P, CHANNELS], F32)
-                nc.tensor.matmul_mx(
-                    out=second[:],
-                    lhsT=prop_codes[:, a, :].bitcast(FP8X4),
-                    lhsT_scale=prop_scales[:, a, :],
-                    rhs=w2_codes[:].bitcast(FP8X4),
-                    rhs_scale=w2_plane[:],
-                    start=True,
-                    stop=True,
-                )
-                nc.vector.tensor_tensor(
-                    out=result[:, a, :], in0=second[:], in1=base_of[u][:, a, :], op=ADD
-                )
-            first = (u % UNITS_PER_CHUNK) * UNIT_BLOCKS
-            nc.sync.dma_start(
-                out=out_v[u // UNITS_PER_CHUNK][:, first : first + UNIT_BLOCKS, :], in_=result[:]
+            nc.vector.quantize_mx(
+                out=prop_codes[:, first:last].rearrange("p a n -> p (a n)").bitcast(FP8X4),
+                scales=prop_scales[:, first:last].rearrange("p a n -> p (a n)"),
+                in_=propg_of[u][:, first:last].rearrange("p a n t -> p (a n t)"),
             )
 
-        for k in range(UNITS + 2):
-            if k < UNITS:
-                transpose_and_quantise(k)
-                if k < 2:
-                    warm_up(2)
-                add_bias_to_residual(k)
-            if 1 <= k <= UNITS:
+        def second_product(u, a):
+            prop_codes, prop_scales = prop_q[u]
+            second = psum_o.tile([P, CHANNELS], F32)
+            nc.tensor.matmul_mx(
+                out=second[:],
+                lhsT=prop_codes[:, a, :].bitcast(FP8X4),
+                lhsT_scale=prop_scales[:, a, :],
+                rhs=w2_codes[:].bitcast(FP8X4),
+                rhs_scale=w2_plane[:],
+                start=True,
+                stop=True,
+            )
+            second_of[u, a] = second
+
+        def finish(u, a):
+            if a == 0:
+                result = late.tile([P, UNIT_BLOCKS, CHANNELS], F32)
+                result_of[u] = result
+            result = result_of[u]
+            nc.vector.tensor_tensor(
+                out=result[:, a, :], in0=second_of[u, a][:], in1=base_of[u][:, a, :], op=ADD
+            )
+
+        def store(u):
+            nc.sync.dma_start(out=part(out_v, u), in_=result_of[u][:])
+
+        def store_block(u, a):
+            nc.sync.dma_start(out=part(out_v, u)[:, a : a + 1], in_=result_of[u][:, a : a + 1])
+
+
+        warm_up([he_raw[:, 0, t] for t in range(4)])
+        spread_bias()
+        group_he(0, 0, 4, nc.vector.tensor_copy)
+        group_he(1, 0, 4, nc.vector.tensor_copy)
+        quantise_he(0, 0, 4)
+        quantise_he(1, 0, 4)
+        for k in range(UNITS):
+            transpose(k)
+            copy_incidence(k)
+            quantise_incidence(k)
+            add_bias_to_residual(k)
+            if k == 0:
+                warm_up([inc_of[0][:, 0, :CHANNELS]] * 2)
+            if k >= 1:
                 first_product(k - 1)
+                copy_prop(k - 1)
+                quantise_prop(k - 1, 0, 2)
             if k >= 2:
-                second_product(k - 2)
+                for a in range(2):
+                    second_product(k - 2, a)
+                    finish(k - 2, a)
+                store(k - 2)
+        last = UNITS - 1
+        first_product(last, [0])
+        open_prop(last)
+        copy_prop_block(last, 0)
+        for a in range(2):
+            second_product(last - 1, a)
+        first_product(last, [1])
+        copy_prop_block(last, 1)
+        finish(last - 1, 0)
+        quantise_prop(last, 0, 1)
+        finish(last - 1, 1)
+        quantise_prop(last, 1, 2)
+        store(last - 1)
+        for a in range(2):
+            second_product(last, a)
+            finish(last, a)
+            store_block(last, a)

@@ -191,12 +191,11 @@ def tile_heterogeneoustemporalhypergraphnn_pb_kernel(
 
         def add_bias_to_residual(u):
             base = late.tile([P, UNIT_BLOCKS, CHANNELS], F32)
-            nc.vector.tensor_tensor(
-                out=base[:],
-                in0=nf_of[u],
-                in1=bias_all[:].unsqueeze(1).to_broadcast([P, UNIT_BLOCKS, CHANNELS]),
-                op=ADD,
-            )
+            engine = nc.gpsimd if u in (3, 5, 7) else nc.vector
+            for a in range(UNIT_BLOCKS):
+                engine.tensor_tensor(
+                    out=base[:, a, :], in0=nf_of[u][:, a, :], in1=bias_all[:], op=ADD
+                )
             base_of[u] = base
 
         def first_product(u, blocks=(0, 1)):

@@ -37,6 +37,7 @@ def tile_heterogeneoustemporalhypergraphnn_pb_kernel(
         inc_pool = ctx.enter_context(tc.tile_pool(name="inc", bufs=UNITS))
         nf_pool = ctx.enter_context(tc.tile_pool(name="nf", bufs=CHUNKS))
         work = ctx.enter_context(tc.tile_pool(name="work", bufs=3))
+        base_pool = ctx.enter_context(tc.tile_pool(name="base", bufs=UNITS))
         late = ctx.enter_context(tc.tile_pool(name="late", bufs=4))
         psum_t = ctx.enter_context(tc.psum_pool(name="psum_t", bufs=2))
         psum_p = ctx.enter_context(tc.psum_pool(name="psum_p", bufs=2))
@@ -96,12 +97,19 @@ def tile_heterogeneoustemporalhypergraphnn_pb_kernel(
         load_he(0)
         load_he(1)
         load_bias()
-        for c in range(CHUNKS):
-            for h in range(UNITS_PER_CHUNK):
-                load_incidence(c * UNITS_PER_CHUNK + h)
-            if c == 0:
-                load_weight()
-            load_features(c)
+        load_incidence(0)
+        load_incidence(1)
+        load_incidence(2)
+        load_features(0)
+        load_weight()
+        load_incidence(3)
+        load_features(1)
+        load_incidence(4)
+        load_incidence(5)
+        load_features(2)
+        load_incidence(6)
+        load_incidence(7)
+        load_features(3)
 
 
         bias_all = keep.tile([P, CHANNELS], F32)
@@ -148,9 +156,9 @@ def tile_heterogeneoustemporalhypergraphnn_pb_kernel(
 
         reordered_of = {}
 
-        def reorder(u, a, copy):
+        def reorder(u, a):
             sorted_words = work.tile([P, EDGE_PASSES, 2, P], F32)
-            copy(
+            nc.scalar.copy(
                 out=sorted_words[:],
                 in_=inc_of[u][:, a, :].bitcast(F32).rearrange("p (g i v) -> p g v i", g=EDGE_PASSES, v=2),
             )
@@ -189,13 +197,18 @@ def tile_heterogeneoustemporalhypergraphnn_pb_kernel(
             )
             inc_q[u] = (codes, scales)
 
-        def add_bias_to_residual(u):
-            base = late.tile([P, UNIT_BLOCKS, CHANNELS], F32)
-            engine = nc.gpsimd if u in (3, 5, 7) else nc.vector
+        def add_bias_to_residual(u, engine, parts):
+            base = base_pool.tile([P, UNIT_BLOCKS, CHANNELS], F32)
+            width = CHANNELS // parts
             for a in range(UNIT_BLOCKS):
-                engine.tensor_tensor(
-                    out=base[:, a, :], in0=nf_of[u][:, a, :], in1=bias_all[:], op=ADD
-                )
+                for h in range(parts):
+                    cols = slice(h * width, (h + 1) * width)
+                    engine.tensor_tensor(
+                        out=base[:, a, cols],
+                        in0=nf_of[u][:, a, cols],
+                        in1=bias_all[:, cols],
+                        op=ADD,
+                    )
             base_of[u] = base
 
         def first_product(u, blocks=(0, 1)):
@@ -278,11 +291,18 @@ def tile_heterogeneoustemporalhypergraphnn_pb_kernel(
         group_he(1, 0, 4, nc.vector.tensor_copy)
         quantise_he(0, 0, 4)
         quantise_he(1, 0, 4)
+        gpsimd_at = {3:3,4:5}
+        vector_at = {0:0,1:1,2:2,4:4,5:6,6:7}
         for k in range(UNITS):
             transpose(k)
             copy_incidence(k)
+            if 2 <= k < UNITS - 1:
+                reorder(k + 1, 0)
             quantise_incidence(k)
-            add_bias_to_residual(k)
+            if k in vector_at:
+                add_bias_to_residual(vector_at[k], nc.vector, 1)
+            if k in gpsimd_at:
+                add_bias_to_residual(gpsimd_at[k], nc.gpsimd, 1)
             if k == 0:
                 warm_up([inc_of[0][:, 0, :CHANNELS]] * 2)
             if k >= 1:

from contextlib import ExitStack

import concourse.mybir as mybir
from concourse.masks import make_identity

BF16 = mybir.dt.bfloat16
F32 = mybir.dt.float32
I32 = mybir.dt.int32
U32 = mybir.dt.uint32
U8 = mybir.dt.uint8
FP8X4 = mybir.dt.float8_e4m3fn_x4
ADD = mybir.AluOpType.add

P = 128
PACK = 4
K_PASS = P * PACK

NODES, EDGES, CHANNELS = 2048, 1024, 512
EDGE_PASSES = EDGES // K_PASS
BLOCK = P
CHUNK_BLOCKS = 4
UNIT_BLOCKS = 2
CHUNKS = NODES // (CHUNK_BLOCKS * BLOCK)
UNITS = NODES // (UNIT_BLOCKS * BLOCK)
UNITS_PER_CHUNK = CHUNK_BLOCKS // UNIT_BLOCKS

FLOPS = 2 * NODES * EDGES * CHANNELS + 2 * NODES * CHANNELS * CHANNELS


def tile_heterogeneoustemporalhypergraphnn_pb_kernel(
    tc, incidence, he, W2_words, W2_scales, b2, node_features, out
):
    nc = tc.nc
    with ExitStack() as ctx:
        ctx.enter_context(tc.manual_schedule())
        keep = ctx.enter_context(tc.tile_pool(name="keep", bufs=1))
        inc_pool = ctx.enter_context(tc.tile_pool(name="inc", bufs=UNITS))
        nf_pool = ctx.enter_context(tc.tile_pool(name="nf", bufs=CHUNKS))
        work = ctx.enter_context(tc.tile_pool(name="work", bufs=3))
        base_pool = ctx.enter_context(tc.tile_pool(name="base", bufs=UNITS))
        late = ctx.enter_context(tc.tile_pool(name="late", bufs=4))
        psum_t = ctx.enter_context(tc.psum_pool(name="psum_t", bufs=2))
        psum_p = ctx.enter_context(tc.psum_pool(name="psum_p", bufs=2))
        psum_o = ctx.enter_context(tc.psum_pool(name="psum_o", bufs=4))

        inc_v = incidence.rearrange("(c p j) e -> c p j e", p=P, j=CHUNK_BLOCKS)
        nf_v = node_features.rearrange("(c p j) n -> c p j n", p=P, j=CHUNK_BLOCKS)
        out_v = out.rearrange("(c p j) n -> c p j n", p=P, j=CHUNK_BLOCKS)
        he_v = he.rearrange("(g p t) n -> g p t n", g=EDGE_PASSES, p=P, t=PACK)

        def part(view, u):
            first = (u % UNITS_PER_CHUNK) * UNIT_BLOCKS
            return view[u // UNITS_PER_CHUNK][:, first : first + UNIT_BLOCKS, :]

        ident = keep.tile([P, P], F32)
        make_identity(nc, ident[:])
        ones = keep.tile([P, P], BF16)
        nc.vector.memset(ones[:], 1.0)
        bias_row = keep.tile([P, CHANNELS], BF16)
        nc.vector.memset(bias_row[:], 0.0)
        w2_plane = keep.tile([P, CHANNELS], U8, align_bytes=64)
        nc.vector.memset(w2_plane[:].bitcast(I32), 0)

        he_raw = keep.tile([P, EDGE_PASSES, PACK, CHANNELS], BF16)
        w2_codes = keep.tile([P, CHANNELS], U32, align_bytes=64)
        inc_of = {}
        nf_of = {}

        def load_incidence(u):
            inc_sb = inc_pool.tile([P, UNIT_BLOCKS, EDGES], BF16)
            nc.sync.dma_start(out=inc_sb[:], in_=part(inc_v, u))
            inc_of[u] = inc_sb

        def load_he(g):
            nc.sync.dma_start(out=he_raw[:, g], in_=he_v[g])

        def load_features(c):
            nf_sb = nf_pool.tile([P, CHUNK_BLOCKS, CHANNELS], BF16)
            nc.sync.dma_start(out=nf_sb[:], in_=nf_v[c])
            for h in range(UNITS_PER_CHUNK):
                nf_of[c * UNITS_PER_CHUNK + h] = nf_sb[:, h * UNIT_BLOCKS : (h + 1) * UNIT_BLOCKS, :]

        def load_weight():
            nc.sync.dma_start(
                out=w2_codes[:].bitcast(I32),
                in_=W2_words[0].rearrange("p n t -> p (n t)").bitcast(I32),
            )
            for quad in range(4):
                nc.sync.dma_start(
                    out=w2_plane[32 * quad : 32 * quad + 4, :].bitcast(I32),
                    in_=W2_scales[0][4 * quad : 4 * quad + 4, :].bitcast(I32),
                )

        def load_bias():
            nc.sync.dma_start(out=bias_row[0:1, :], in_=b2.rearrange("(o n) -> o n", o=1))

        load_he(0)
        load_he(1)
        load_bias()
        load_incidence(0)
        load_incidence(1)
        load_incidence(2)
        load_features(0)
        load_weight()
        load_incidence(3)
        load_features(1)
        load_incidence(4)
        load_incidence(5)
        load_features(2)
        load_incidence(6)
        load_incidence(7)
        load_features(3)


        bias_all = keep.tile([P, CHANNELS], F32)

        def spread_bias():
            bias_ps = psum_o.tile([P, CHANNELS], F32, tag="second")
            nc.tensor.matmul(
                out=bias_ps[:], lhsT=ones[:], rhs=bias_row[:], start=True, stop=True
            )
            nc.scalar.copy(out=bias_all[:], in_=bias_ps[:])

        def warm_up(rows):
            for row in rows:
                idle = psum_o.tile([P, CHANNELS], F32, tag="second")
                nc.tensor.matmul(out=idle[:], lhsT=ones[:], rhs=row, start=True, stop=True)

        he_grouped = keep.tile([P, EDGE_PASSES, PACK, P, PACK], BF16, align_bytes=64)
        he_codes = keep.tile([P, EDGE_PASSES, CHANNELS], U32, align_bytes=64)
        he_scales = keep.tile([P, EDGE_PASSES, CHANNELS], U8, align_bytes=64)

        def group_he(g, first, last, copy):
            copy(
                out=he_grouped[:, g, first:last].rearrange("p q m t -> p m t q"),
                in_=he_raw[:, g].rearrange("p t (m q) -> p m t q", q=PACK)[:, :, :, first:last],
            )

        def quantise_he(g, first, last):
            cols = slice(first * P, last * P)
            nc.vector.quantize_mx(
                out=he_codes[:, g, cols].bitcast(FP8X4),
                scales=he_scales[:, g, cols],
                in_=he_grouped[:, g, first:last].rearrange("p q m t -> p (q m t)"),
            )

        flipped_of = {}
        grouped_of = {}
        inc_q = {}
        prop_ps_of = {}
        propg_of = {}
        prop_q = {}
        base_of = {}
        second_of = {}
        result_of = {}

        reordered_of = {}

        def reorder(u, a):
            sorted_words = work.tile([P, EDGE_PASSES, 2, P], F32)
            nc.scalar.copy(
                out=sorted_words[:],
                in_=inc_of[u][:, a, :].bitcast(F32).rearrange("p (g i v) -> p g v i", g=EDGE_PASSES, v=2),
            )
            reordered_of[u, a] = sorted_words

        def transpose(u):
            for a in range(UNIT_BLOCKS):
                words = inc_of[u][:, a, :].bitcast(F32)
                flipped = psum_t.tile([P, EDGE_PASSES * 2, BLOCK], F32)
                for g in range(EDGE_PASSES):
                    for v in range(2):
                        if (u, a) in reordered_of:
                            source = reordered_of[u, a][:, g, v, :]
                        else:
                            source = words[:, 2 * P * g + v : 2 * P * (g + 1) : 2]
                        nc.tensor.transpose(flipped[:, 2 * g + v, :], source, ident[:])
                flipped_of[u, a] = flipped

        def copy_incidence(u):
            grouped = work.tile([P, UNIT_BLOCKS, EDGE_PASSES, BLOCK, PACK], BF16, align_bytes=64)
            for a in range(UNIT_BLOCKS):
                nc.scalar.copy(
                    out=grouped[:, a].bitcast(F32),
                    in_=flipped_of[u, a][:].rearrange("p (g u) n -> p g n u", u=2),
                )
            grouped_of[u] = grouped

        def quantise_incidence(u):
            grouped = grouped_of[u]
            codes = work.tile([P, UNIT_BLOCKS, EDGE_PASSES, BLOCK], U32, align_bytes=64)
            scales = work.tile([P, UNIT_BLOCKS, EDGE_PASSES, BLOCK], U8, align_bytes=64)
            nc.vector.quantize_mx(
                out=codes[:].rearrange("p a g n -> p (a g n)").bitcast(FP8X4),
                scales=scales[:].rearrange("p a g n -> p (a g n)"),
                in_=grouped[:].rearrange("p a g n t -> p (a g n t)"),
            )
            inc_q[u] = (codes, scales)

        def add_bias_to_residual(u, engine, parts):
            base = base_pool.tile([P, UNIT_BLOCKS, CHANNELS], F32)
            width = CHANNELS // parts
            for a in range(UNIT_BLOCKS):
                for h in range(parts):
                    cols = slice(h * width, (h + 1) * width)
                    engine.tensor_tensor(
                        out=base[:, a, cols],
                        in0=nf_of[u][:, a, cols],
                        in1=bias_all[:, cols],
                        op=ADD,
                    )
            base_of[u] = base

        def first_product(u, blocks=(0, 1)):
            codes, scales = inc_q[u]
            for a in blocks:
                prop_ps = psum_p.tile([P, PACK, BLOCK], F32)
                for q in range(PACK):
                    cols = slice(q * P, (q + 1) * P)
                    for g in range(EDGE_PASSES):
                        nc.tensor.matmul_mx(
                            out=prop_ps[:, q, :],
                            lhsT=he_codes[:, g, cols].bitcast(FP8X4),
                            lhsT_scale=he_scales[:, g, cols],
                            rhs=codes[:, a, g, :].bitcast(FP8X4),
                            rhs_scale=scales[:, a, g, :],
                            start=(g == 0),
                            stop=(g == EDGE_PASSES - 1),
                        )
                prop_ps_of[u, a] = prop_ps

        def copy_prop(u):
            open_prop(u)
            for a in range(UNIT_BLOCKS):
                copy_prop_block(u, a)

        def copy_prop_block(u, a):
            nc.scalar.copy(
                out=propg_of[u][:, a],
                in_=prop_ps_of[u, a][:].rearrange("p q n -> p n q"),
            )

        def open_prop(u):
            prop_grouped = work.tile([P, UNIT_BLOCKS, BLOCK, PACK], BF16, align_bytes=64)
            propg_of[u] = prop_grouped
            prop_codes = work.tile([P, UNIT_BLOCKS, BLOCK], U32, align_bytes=64)
            prop_scales = work.tile([P, UNIT_BLOCKS, BLOCK], U8, align_bytes=64)
            prop_q[u] = (prop_codes, prop_scales)

        def quantise_prop(u, first, last):
            prop_codes, prop_scales = prop_q[u]
            nc.vector.quantize_mx(
                out=prop_codes[:, first:last].rearrange("p a n -> p (a n)").bitcast(FP8X4),
                scales=prop_scales[:, first:last].rearrange("p a n -> p (a n)"),
                in_=propg_of[u][:, first:last].rearrange("p a n t -> p (a n t)"),
            )

        def second_product(u, a):
            prop_codes, prop_scales = prop_q[u]
            second = psum_o.tile([P, CHANNELS], F32)
            nc.tensor.matmul_mx(
                out=second[:],
                lhsT=prop_codes[:, a, :].bitcast(FP8X4),
                lhsT_scale=prop_scales[:, a, :],
                rhs=w2_codes[:].bitcast(FP8X4),
                rhs_scale=w2_plane[:],
                start=True,
                stop=True,
            )
            second_of[u, a] = second

        def finish(u, a):
            if a == 0:
                result = late.tile([P, UNIT_BLOCKS, CHANNELS], F32)
                result_of[u] = result
            result = result_of[u]
            nc.vector.tensor_tensor(
                out=result[:, a, :], in0=second_of[u, a][:], in1=base_of[u][:, a, :], op=ADD
            )

        def store(u):
            nc.sync.dma_start(out=part(out_v, u), in_=result_of[u][:])

        def store_block(u, a):
            nc.sync.dma_start(out=part(out_v, u)[:, a : a + 1], in_=result_of[u][:, a : a + 1])


        warm_up([he_raw[:, 0, t] for t in range(4)])
        spread_bias()
        group_he(0, 0, 4, nc.vector.tensor_copy)
        group_he(1, 0, 4, nc.vector.tensor_copy)
        quantise_he(0, 0, 4)
        quantise_he(1, 0, 4)
        gpsimd_at = {3:3,4:5}
        vector_at = {0:0,1:1,2:2,4:4,5:6,6:7}
        for k in range(UNITS):
            transpose(k)
            copy_incidence(k)
            if 2 <= k < UNITS - 1:
                reorder(k + 1, 0)
            quantise_incidence(k)
            if k in vector_at:
                add_bias_to_residual(vector_at[k], nc.vector, 1)
            if k in gpsimd_at:
                add_bias_to_residual(gpsimd_at[k], nc.gpsimd, 1)
            if k == 0:
                warm_up([inc_of[0][:, 0, :CHANNELS]] * 2)
            if k >= 1:
                first_product(k - 1)
                copy_prop(k - 1)
                quantise_prop(k - 1, 0, 2)
            if k >= 2:
                for a in range(2):
                    second_product(k - 2, a)
                    finish(k - 2, a)
                store(k - 2)
        last = UNITS - 1
        first_product(last, [0])
        open_prop(last)
        copy_prop_block(last, 0)
        for a in range(2):
            second_product(last - 1, a)
        first_product(last, [1])
        copy_prop_block(last, 1)
        finish(last - 1, 0)
        quantise_prop(last, 0, 1)
        finish(last - 1, 1)
        quantise_prop(last, 1, 2)
        store(last - 1)
        for a in range(2):
            second_product(last, a)
            finish(last, a)
            store_block(last, a)
